import numpy as np
import ml_dtypes


def mxq(x, axis, fmt="e4m3"):
    dtype, down = {"e4m3": (ml_dtypes.float8_e4m3fn, 7), "e5m2": (ml_dtypes.float8_e5m2, 14)}[fmt]
    v = np.moveaxis(np.asarray(x, np.float32).astype(ml_dtypes.bfloat16).astype(np.float64), axis, -1)
    blocks = v.reshape(v.shape[:-1] + (-1, 32))
    amax = np.abs(blocks).max(-1, keepdims=True)
    byte = np.maximum(np.where(amax > 0, np.frexp(amax)[1] - 1 + 127, 0) - down, 1)
    scale = np.exp2(byte - 127.0)
    codes = (blocks / scale).astype(np.float32).astype(dtype).astype(np.float64)
    return np.moveaxis((codes * scale).reshape(v.shape), -1, axis)


WIDE = False


def mx_kscale(k):
    if not WIDE:
        return np.ones(k)
    levels = np.array([30, -30])
    if k % 512:
        return np.exp2(np.random.permutation(np.resize(levels, k // 32))).repeat(32)
    a = np.empty((k // 512, 16))
    for p in range(k // 512):
        a[p, :8] = np.random.permutation(np.resize(levels, 8))
        for g in range(8):
            far = levels[np.abs(levels - a[p, g]) >= 10]
            a[p, g + 8] = far[np.random.randint(len(far))]
    return np.exp2(a.ravel()).repeat(32)


BF16 = ml_dtypes.bfloat16


def bf(x):
    return np.asarray(x, np.float32).astype(BF16)


def f64(x):
    return np.asarray(x).astype(np.float64)


B, S, D, E, Q = 2, 1024, 512, 512, 512
P = S - Q


def setup_inputs():
    s = mx_kscale(E)
    return {"q_rot": bf(np.random.standard_normal((B, Q, E)) * s),
            "k_rot": bf(np.random.standard_normal((B, S, E)) / s)}


def reference(q_rot, k_rot):
    scores = (mxq(f64(q_rot), 2, "e5m2") @ mxq(f64(k_rot), 2, "e4m3").transpose(0, 2, 1)) / np.sqrt(E)
    mask = np.triu(np.full((Q, S), -np.inf), 1 + P)
    scores = scores + mask
    e = np.exp(scores - scores.max(-1, keepdims=True))
    return e / e.sum(-1, keepdims=True)

@@ -1,0 +1,263 @@
+import math
+from contextlib import ExitStack
+
+import concourse.mybir as mybir
+from concourse.masks import make_identity
+
+B, S, E, Q = 2, 1024, 512, 512
+P = 128
+CHUNK = 256
+FIRST = S - Q
+BANK = 512
+N_BANKS = 8
+BIG = 2.0 ** 127
+FLOPS = 2 * B * Q * S * E
+
+F32 = mybir.dt.float32
+BF16 = mybir.dt.bfloat16
+U32 = mybir.dt.uint32
+U8 = mybir.dt.uint8
+E5M2 = mybir.dt.float8_e5m2_x4
+E4M3 = mybir.dt.float8_e4m3fn_x4
+ALU = mybir.AluOpType
+ACT = mybir.ActivationFunctionType
+NEG_SCALE = -1.0 / math.sqrt(E)
+
+
+def tile_rawattention_pb_kernel(tc, q_rot, k_rot, out):
+    nc = tc.nc
+    with ExitStack() as ctx:
+        keep = ctx.enter_context(tc.tile_pool(name="keep", bufs=1))
+        psum = ctx.enter_context(tc.psum_pool(name="psum", bufs=1))
+        ctx.enter_context(tc.manual_schedule())
+
+        banks_taken = []
+
+        def next_bank():
+            name = "bank%d" % (len(banks_taken) % N_BANKS)
+            bank = psum.tile([P, BANK], F32, name=name, tag=name)
+            banks_taken.append(name)
+            return bank
+
+        chunks = [("q", 0, 0), ("k", 0, 2), ("k", 0, 0), ("k", 0, 1), ("q", 0, 1), ("k", 0, 3),
+                  ("q", 1, 1), ("k", 1, 3), ("k", 1, 2), ("k", 1, 0), ("k", 1, 1), ("q", 1, 0)]
+        pairs = [(0, 0), (0, 1), (1, 1), (1, 0)]
+
+        raw = []
+        for n, (kind, b, c) in enumerate(chunks):
+            rows = (q_rot if kind == "q" else k_rot)[b, c * CHUNK:(c + 1) * CHUNK, :]
+            t = keep.tile([P, 2, E], BF16, name="raw%d" % n)
+            nc.sync.dma_start(out=t[:], in_=rows.rearrange("(p j) e -> p j e", j=2))
+            raw.append(t)
+
+        ident = keep.tile([P, P], F32, name="ident")
+        make_identity(nc, ident[:])
+        mask = keep.tile([P, 2, P], F32, name="mask")
+        nc.gpsimd.memset(mask[:], -BIG)
+        nc.gpsimd.affine_select(out=mask[:], in_=mask[:], pattern=[[0, 2], [-1, P]], compare_op=ALU.is_ge,
+                                fill=BIG, base=0, channel_multiplier=1)
+
+        widest = Q - P
+        masked = keep.tile([P, B, widest], F32, name="masked")
+        nc.vector.memset(masked[:], BIG)
+        zeros = keep.tile([P, B, widest], F32, name="zeros")
+        nc.scalar.activation(out=zeros[:], in_=masked[:], func=ACT.Exp, scale=-1.0)
+        for i in range(Q // P - 1):
+            seen = FIRST + (i + 1) * P
+            nc.sync.dma_start(out=out[:, i * P:(i + 1) * P, seen:].rearrange("b p n -> p b n"),
+                              in_=zeros[:, :, :S - seen])
+
+        codes = {}
+        scales = {}
+        for b in range(B):
+            for kind, rows in (("q", Q), ("k", S)):
+                codes[kind, b] = keep.tile([P, rows], U32, name="codes_%s%d" % (kind, b), align_bytes=64)
+                scales[kind, b] = keep.tile([P, rows], U8, name="scales_%s%d" % (kind, b), align_bytes=64)
+
+        grouped = {}
+
+        def turn(n, on_vector=False):
+            words = raw[n][:].bitcast(F32)
+            bank = next_bank()
+            for j in range(2):
+                for u in range(2):
+                    a = 2 * j + u
+                    nc.tensor.transpose(bank[:, a * P:(a + 1) * P], words[:, j, u::2], ident[:])
+            g = keep.tile([P, 4 * CHUNK], BF16, name="grouped%d" % n, align_bytes=64)
+            dst = g[:].bitcast(F32).rearrange("p (r a) -> p r a", a=4)
+            src = bank[:].rearrange("p (a r) -> p r a", a=4)
+            if on_vector:
+                nc.vector.tensor_copy(out=dst, in_=src)
+            else:
+                nc.scalar.copy(out=dst, in_=src)
+            grouped[n] = g
+
+        def quantize(n):
+            kind, b, c = chunks[n]
+            cols = slice(c * CHUNK, (c + 1) * CHUNK)
+            nc.vector.quantize_mx(out=codes[kind, b][:, cols].bitcast(E5M2 if kind == "q" else E4M3),
+                                  scales=scales[kind, b][:, cols], in_=grouped[n][:])
+
+        def scores(dst, b, i, key0, width):
+            qs = slice(i * P, (i + 1) * P)
+            ks = slice(key0, key0 + width)
+            nc.tensor.matmul_mx(out=dst, lhsT=codes["q", b][:, qs].bitcast(E5M2), lhsT_scale=scales["q", b][:, qs],
+                                rhs=codes["k", b][:, ks].bitcast(E4M3), rhs_scale=scales["k", b][:, ks],
+                                start=True, stop=True)
+
+        neg = [keep.tile([P, 2, S], F32, name="neg%d" % n) for n in range(4)]
+        prob = [keep.tile([P, 2, S], F32, name="prob%d" % n) for n in range(4)]
+        low = [keep.tile([P, 3, 2], F32, name="low%d" % n) for n in range(4)]
+        total = [keep.tile([P, 2], F32, name="total%d" % n) for n in range(4)]
+        inv = [keep.tile([P, 2], F32, name="inv%d" % n) for n in range(4)]
+        diag, mid, far = {}, {}, {}
+
+        def seen(n, j):
+            return FIRST + (2 * pairs[n][1] + j + 1) * P
+
+        def near_scores(n):
+            b, h = pairs[n]
+            bank = next_bank()
+            for j in range(2):
+                scores(bank[:, j * P:(j + 1) * P], b, 2 * h + j, seen(n, j) - P, P)
+            diag[n] = bank
+            used = 2 * P
+            for j in range(2):
+                width = seen(n, j) - P - FIRST
+                if width == 0:
+                    continue
+                if used + width > BANK:
+                    bank = next_bank()
+                    used = 0
+                done = 0
+                for piece in (2 * P, P):
+                    if width - done >= piece:
+                        scores(bank[:, used + done:used + done + piece], b, 2 * h + j, FIRST + done, piece)
+                        done += piece
+                mid[n, j] = bank[:, used:used + width]
+                used += width
+
+        def far_scores(n, order=(0, 1)):
+            b, h = pairs[n]
+            for j in order:
+                bank = next_bank()
+                scores(bank[:], b, 2 * h + j, 0, FIRST)
+                far[n, j] = bank
+
+        def mask_diag(n):
+            nc.vector.scalar_tensor_tensor(out=neg[n][:, :, S - P:], in0=diag[n][:, :2 * P].rearrange("p (j c) -> p j c", j=2),
+                                           scalar=NEG_SCALE, in1=mask[:], op0=ALU.mult, op1=ALU.max)
+
+        def min_diag(n):
+            nc.vector.tensor_reduce(out=low[n][:, 0, :], in_=neg[n][:, :, S - P:], axis=mybir.AxisListType.X, op=ALU.min)
+
+        def min_mid(n, j):
+            start = S - seen(n, j) + FIRST
+            nc.vector.tensor_scalar(out=neg[n][:, j, start:S - P], in0=mid[n, j], scalar1=NEG_SCALE,
+                                    scalar2=low[n][:, 0, j:j + 1], op0=ALU.mult, op1=ALU.min,
+                                    accum_out=low[n][:, 1, j:j + 1])
+
+        def min_far(n, j):
+            start = S - seen(n, j)
+            before = 1 if (n, j) in mid else 0
+            nc.vector.tensor_scalar(out=neg[n][:, j, start:start + FIRST], in0=far[n, j][:], scalar1=NEG_SCALE,
+                                    scalar2=low[n][:, before, j:j + 1], op0=ALU.mult, op1=ALU.min,
+                                    accum_out=low[n][:, 2, j:j + 1])
+
+        def exp(n, j):
+            w = seen(n, j)
+            nc.scalar.activation(out=prob[n][:, j, :w], in_=neg[n][:, j, S - w:], func=ACT.Exp, scale=-1.0,
+                                 bias=low[n][:, 2, j:j + 1], accum_out=total[n][:, j:j + 1])
+
+        def invert(n, js):
+            nc.vector.reciprocal(out=inv[n][:, js], in_=total[n][:, js])
+
+        def finish(n, j, on_vector=False):
+            b, h = pairs[n]
+            w = seen(n, j)
+            row = prob[n][:, j, :w]
+            if on_vector:
+                nc.vector.tensor_scalar(out=row, in0=row, scalar1=inv[n][:, j:j + 1], scalar2=None, op0=ALU.mult)
+            else:
+                nc.gpsimd.tensor_scalar(out=row, in0=row, scalar1=inv[n][:, j:j + 1], scalar2=0.0,
+                                        op0=ALU.mult, op1=ALU.add)
+            i = 2 * h + j
+            nc.sync.dma_start(out=out[b, i * P:(i + 1) * P, :w], in_=row)
+
+        both = slice(0, 2)
+        turn(0, on_vector=True)
+        turn(1)
+        quantize(0)
+        turn(2)
+        quantize(1)
+        turn(3)
+        quantize(2)
+        turn(4)
+        near_scores(0)
+        mask_diag(0)
+        quantize(3)
+        turn(5)
+        far_scores(0)
+        min_diag(0)
+        quantize(4)
+        min_mid(0, 1)
+        turn(6)
+        quantize(5)
+        turn(7)
+        near_scores(1)
+        min_far(0, 0)
+        exp(0, 0)
+        mask_diag(1)
+        min_far(0, 1)
+        exp(0, 1)
+        min_diag(1)
+        far_scores(1)
+        turn(8)
+        turn(9)
+        quantize(6)
+        quantize(7)
+        invert(0, both)
+        finish(0, 0)
+        finish(0, 1)
+        min_mid(1, 0)
+        min_mid(1, 1)
+        turn(10)
+        turn(11)
+        min_far(1, 0)
+        exp(1, 0)
+        min_far(1, 1)
+        exp(1, 1)
+        quantize(8)
+        quantize(9)
+        near_scores(2)
+        mask_diag(2)
+        quantize(10)
+        far_scores(2)
+        min_diag(2)
+        quantize(11)
+        near_scores(3)
+        invert(1, both)
+        finish(1, 0)
+        finish(1, 1)
+        min_mid(2, 0)
+        min_mid(2, 1)
+        mask_diag(3)
+        far_scores(3, (1, 0))
+        min_far(2, 0)
+        exp(2, 0)
+        min_diag(3)
+        min_far(2, 1)
+        exp(2, 1)
+        min_mid(3, 1)
+        invert(2, slice(0, 1))
+        finish(2, 0)
+        min_far(3, 1)
+        exp(3, 1)
+        min_far(3, 0)
+        exp(3, 0)
+        invert(2, slice(1, 2))
+        finish(2, 1, on_vector=True)
+        invert(3, slice(1, 2))
+        finish(3, 1, on_vector=True)
+        invert(3, slice(0, 1))
+        finish(3, 0, on_vector=True)

@@ -31,12 +31,8 @@ def tile_rawattention_pb_kernel(tc, q_rot, k_rot, out):
         psum = ctx.enter_context(tc.psum_pool(name="psum", bufs=1))
         ctx.enter_context(tc.manual_schedule())
 
-        banks_taken = []
-
         def next_bank():
-            name = "bank%d" % (len(banks_taken) % N_BANKS)
-            bank = psum.tile([P, BANK], F32, name=name, tag=name)
-            banks_taken.append(name)
+            bank = psum.tile([P, BANK], F32, name="bank", bufs=N_BANKS)
             return bank
 
         chunks = [("q", 0, 0), ("k", 0, 2), ("k", 0, 0), ("k", 0, 1), ("q", 0, 1), ("k", 0, 3),
@@ -194,70 +190,76 @@ def tile_rawattention_pb_kernel(tc, q_rot, k_rot, out):
         quantize(2)
         turn(4)
         near_scores(0)
-        mask_diag(0)
         quantize(3)
-        turn(5)
-        far_scores(0)
-        min_diag(0)
+        far_scores(0, (0,))
+        far_scores(0, (1,))
+        mask_diag(0)
         quantize(4)
-        min_mid(0, 1)
+        min_diag(0)
+        turn(5)
         turn(6)
-        quantize(5)
         turn(7)
-        near_scores(1)
+        min_mid(0, 1)
         min_far(0, 0)
         exp(0, 0)
-        mask_diag(1)
         min_far(0, 1)
         exp(0, 1)
+        quantize(5)
+        near_scores(1)
+        far_scores(1, (0,))
+        far_scores(1, (1,))
+        quantize(6)
+        mask_diag(1)
+        quantize(7)
         min_diag(1)
-        far_scores(1)
+        invert(0, slice(0, 1))
+        finish(0, 0)
         turn(8)
         turn(9)
-        quantize(6)
-        quantize(7)
-        invert(0, both)
-        finish(0, 0)
-        finish(0, 1)
-        min_mid(1, 0)
-        min_mid(1, 1)
         turn(10)
         turn(11)
+        min_mid(1, 0)
+        min_mid(1, 1)
+        invert(0, slice(1, 2))
+        finish(0, 1)
         min_far(1, 0)
         exp(1, 0)
         min_far(1, 1)
         exp(1, 1)
         quantize(8)
-        quantize(9)
         near_scores(2)
-        mask_diag(2)
+        quantize(9)
         quantize(10)
-        far_scores(2)
-        min_diag(2)
+        far_scores(2, (0,))
+        far_scores(2, (1,))
+        mask_diag(2)
         quantize(11)
         near_scores(3)
-        invert(1, both)
+        min_diag(2)
+        invert(1, slice(0, 1))
         finish(1, 0)
-        finish(1, 1)
         min_mid(2, 0)
         min_mid(2, 1)
-        mask_diag(3)
-        far_scores(3, (1, 0))
+        invert(1, slice(1, 2))
+        finish(1, 1)
         min_far(2, 0)
         exp(2, 0)
-        min_diag(3)
+        mask_diag(3)
         min_far(2, 1)
         exp(2, 1)
-        min_mid(3, 1)
+        min_diag(3)
+        far_scores(3, (1,))
+        far_scores(3, (0,))
         invert(2, slice(0, 1))
         finish(2, 0)
-        min_far(3, 1)
-        exp(3, 1)
+        min_mid(3, 1)
         min_far(3, 0)
         exp(3, 0)
+        min_far(3, 1)
+        exp(3, 1)
         invert(2, slice(1, 2))
         finish(2, 1, on_vector=True)
-        invert(3, slice(1, 2))
-        finish(3, 1, on_vector=True)
         invert(3, slice(0, 1))
         finish(3, 0, on_vector=True)
+        invert(3, slice(1, 2))
+        finish(3, 1, on_vector=True)

@@ -5,23 +5,33 @@ import concourse.mybir as mybir
 from concourse.masks import make_identity
 
 B, S, E, Q = 2, 1024, 512, 512
+FLOPS = 2 * B * Q * S * E
+
 P = 128
 CHUNK = 256
-FIRST = S - Q
+FAR = S - Q
 BANK = 512
 N_BANKS = 8
-BIG = 2.0 ** 127
-FLOPS = 2 * B * Q * S * E
+HUGE = 2.0 ** 127
+NEG_SCALE = -1.0 / math.sqrt(E)
 
 F32 = mybir.dt.float32
 BF16 = mybir.dt.bfloat16
 U32 = mybir.dt.uint32
 U8 = mybir.dt.uint8
-E5M2 = mybir.dt.float8_e5m2_x4
-E4M3 = mybir.dt.float8_e4m3fn_x4
+FORMAT = {"q": mybir.dt.float8_e5m2_x4, "k": mybir.dt.float8_e4m3fn_x4}
 ALU = mybir.AluOpType
 ACT = mybir.ActivationFunctionType
-NEG_SCALE = -1.0 / math.sqrt(E)
+
+PAIRS = [(0, 0), (0, 1), (1, 1), (1, 0)]
+CHUNKS = [("q", 0, 0), ("k", 0, 2), ("k", 0, 0), ("k", 0, 1),
+          ("q", 0, 1), ("k", 0, 3),
+          ("q", 1, 1), ("k", 1, 3), ("k", 1, 2), ("k", 1, 0), ("k", 1, 1),
+          ("q", 1, 0)]
+
+
+def seen(n, j):
+    return FAR + (2 * PAIRS[n][1] + j + 1) * P
 
 
 def tile_rawattention_pb_kernel(tc, q_rot, k_rot, out):
@@ -35,91 +45,84 @@ def tile_rawattention_pb_kernel(tc, q_rot, k_rot, out):
             bank = psum.tile([P, BANK], F32, name="bank", bufs=N_BANKS)
             return bank
 
-        chunks = [("q", 0, 0), ("k", 0, 2), ("k", 0, 0), ("k", 0, 1), ("q", 0, 1), ("k", 0, 3),
-                  ("q", 1, 1), ("k", 1, 3), ("k", 1, 2), ("k", 1, 0), ("k", 1, 1), ("q", 1, 0)]
-        pairs = [(0, 0), (0, 1), (1, 1), (1, 0)]
-
         raw = []
-        for n, (kind, b, c) in enumerate(chunks):
-            rows = (q_rot if kind == "q" else k_rot)[b, c * CHUNK:(c + 1) * CHUNK, :]
-            t = keep.tile([P, 2, E], BF16, name="raw%d" % n)
-            nc.sync.dma_start(out=t[:], in_=rows.rearrange("(p j) e -> p j e", j=2))
-            raw.append(t)
+        for c, (kind, b, part) in enumerate(CHUNKS):
+            rows = (q_rot if kind == "q" else k_rot)[b, part * CHUNK:(part + 1) * CHUNK, :]
+            loaded = keep.tile([P, 2, E], BF16, name="raw%d" % c)
+            nc.sync.dma_start(out=loaded[:], in_=rows.rearrange("(p r) e -> p r e", r=2))
+            raw.append(loaded)
 
         ident = keep.tile([P, P], F32, name="ident")
         make_identity(nc, ident[:])
         mask = keep.tile([P, 2, P], F32, name="mask")
-        nc.gpsimd.memset(mask[:], -BIG)
+        nc.gpsimd.memset(mask[:], -HUGE)
         nc.gpsimd.affine_select(out=mask[:], in_=mask[:], pattern=[[0, 2], [-1, P]], compare_op=ALU.is_ge,
-                                fill=BIG, base=0, channel_multiplier=1)
+                                fill=HUGE, base=0, channel_multiplier=1)
 
-        widest = Q - P
+        widest = S - FAR - P
         masked = keep.tile([P, B, widest], F32, name="masked")
-        nc.vector.memset(masked[:], BIG)
+        nc.vector.memset(masked[:], HUGE)
         zeros = keep.tile([P, B, widest], F32, name="zeros")
         nc.scalar.activation(out=zeros[:], in_=masked[:], func=ACT.Exp, scale=-1.0)
         for i in range(Q // P - 1):
-            seen = FIRST + (i + 1) * P
-            nc.sync.dma_start(out=out[:, i * P:(i + 1) * P, seen:].rearrange("b p n -> p b n"),
-                              in_=zeros[:, :, :S - seen])
+            first_zero = FAR + (i + 1) * P
+            nc.sync.dma_start(out=out[:, i * P:(i + 1) * P, first_zero:].rearrange("b p n -> p b n"),
+                              in_=zeros[:, :, :S - first_zero])
 
         codes = {}
         scales = {}
         for b in range(B):
-            for kind, rows in (("q", Q), ("k", S)):
-                codes[kind, b] = keep.tile([P, rows], U32, name="codes_%s%d" % (kind, b), align_bytes=64)
-                scales[kind, b] = keep.tile([P, rows], U8, name="scales_%s%d" % (kind, b), align_bytes=64)
+            for kind, n_rows in (("q", Q), ("k", S)):
+                codes[kind, b] = keep.tile([P, n_rows], U32, name="codes_%s%d" % (kind, b), align_bytes=64)
+                scales[kind, b] = keep.tile([P, n_rows], U8, name="scales_%s%d" % (kind, b), align_bytes=64)
 
         grouped = {}
 
-        def turn(n, on_vector=False):
-            words = raw[n][:].bitcast(F32)
+        def transpose_chunk(c, copy):
+            words = raw[c][:].bitcast(F32)
             bank = next_bank()
-            for j in range(2):
+            for r in range(2):
                 for u in range(2):
-                    a = 2 * j + u
-                    nc.tensor.transpose(bank[:, a * P:(a + 1) * P], words[:, j, u::2], ident[:])
-            g = keep.tile([P, 4 * CHUNK], BF16, name="grouped%d" % n, align_bytes=64)
-            dst = g[:].bitcast(F32).rearrange("p (r a) -> p r a", a=4)
-            src = bank[:].rearrange("p (a r) -> p r a", a=4)
-            if on_vector:
-                nc.vector.tensor_copy(out=dst, in_=src)
-            else:
-                nc.scalar.copy(out=dst, in_=src)
-            grouped[n] = g
+                    slot = 2 * r + u
+                    nc.tensor.transpose(bank[:, slot * P:(slot + 1) * P], words[:, r, u::2], ident[:])
+            turned = keep.tile([P, 4 * CHUNK], BF16, name="grouped%d" % c, align_bytes=64)
+            copy(out=turned[:].bitcast(F32).rearrange("p (m slot) -> p m slot", slot=4),
+                 in_=bank[:].rearrange("p (slot m) -> p m slot", slot=4))
+            grouped[c] = turned
 
-        def quantize(n):
-            kind, b, c = chunks[n]
-            cols = slice(c * CHUNK, (c + 1) * CHUNK)
-            nc.vector.quantize_mx(out=codes[kind, b][:, cols].bitcast(E5M2 if kind == "q" else E4M3),
-                                  scales=scales[kind, b][:, cols], in_=grouped[n][:])
+        def quantize(c):
+            kind, b, part = CHUNKS[c]
+            cols = slice(part * CHUNK, (part + 1) * CHUNK)
+            nc.vector.quantize_mx(out=codes[kind, b][:, cols].bitcast(FORMAT[kind]),
+                                  scales=scales[kind, b][:, cols], in_=grouped[c][:])
 
-        def scores(dst, b, i, key0, width):
-            qs = slice(i * P, (i + 1) * P)
-            ks = slice(key0, key0 + width)
-            nc.tensor.matmul_mx(out=dst, lhsT=codes["q", b][:, qs].bitcast(E5M2), lhsT_scale=scales["q", b][:, qs],
-                                rhs=codes["k", b][:, ks].bitcast(E4M3), rhs_scale=scales["k", b][:, ks],
+        def scores(dst, n, j, key0, width):
+            b, part = PAIRS[n]
+            queries = slice(part * CHUNK + j * P, part * CHUNK + (j + 1) * P)
+            keys = slice(key0, key0 + width)
+            nc.tensor.matmul_mx(out=dst,
+                                lhsT=codes["q", b][:, queries].bitcast(FORMAT["q"]),
+                                lhsT_scale=scales["q", b][:, queries],
+                                rhs=codes["k", b][:, keys].bitcast(FORMAT["k"]),
+                                rhs_scale=scales["k", b][:, keys],
                                 start=True, stop=True)
 
-        neg = [keep.tile([P, 2, S], F32, name="neg%d" % n) for n in range(4)]
-        prob = [keep.tile([P, 2, S], F32, name="prob%d" % n) for n in range(4)]
-        low = [keep.tile([P, 3, 2], F32, name="low%d" % n) for n in range(4)]
-        total = [keep.tile([P, 2], F32, name="total%d" % n) for n in range(4)]
-        inv = [keep.tile([P, 2], F32, name="inv%d" % n) for n in range(4)]
-        diag, mid, far = {}, {}, {}
-
-        def seen(n, j):
-            return FIRST + (2 * pairs[n][1] + j + 1) * P
+        pairs = range(len(PAIRS))
+        neg = [keep.tile([P, 2, S], F32, name="neg%d" % n) for n in pairs]
+        prob = [keep.tile([P, 2, S], F32, name="prob%d" % n) for n in pairs]
+        least = [keep.tile([P, 3, 2], F32, name="least%d" % n) for n in pairs]
+        total = [keep.tile([P, 2], F32, name="total%d" % n) for n in pairs]
+        inverse = [keep.tile([P, 2], F32, name="inverse%d" % n) for n in pairs]
+        diagonal, middle, far = {}, {}, {}
 
         def near_scores(n):
-            b, h = pairs[n]
             bank = next_bank()
             for j in range(2):
-                scores(bank[:, j * P:(j + 1) * P], b, 2 * h + j, seen(n, j) - P, P)
-            diag[n] = bank
+                scores(bank[:, j * P:(j + 1) * P], n, j, seen(n, j) - P, P)
+            diagonal[n] = bank
             used = 2 * P
             for j in range(2):
-                width = seen(n, j) - P - FIRST
+                width = seen(n, j) - P - FAR
                 if width == 0:
                     continue
                 if used + width > BANK:
@@ -128,138 +131,139 @@ def tile_rawattention_pb_kernel(tc, q_rot, k_rot, out):
                 done = 0
                 for piece in (2 * P, P):
                     if width - done >= piece:
-                        scores(bank[:, used + done:used + done + piece], b, 2 * h + j, FIRST + done, piece)
+                        scores(bank[:, used + done:used + done + piece], n, j, FAR + done, piece)
                         done += piece
-                mid[n, j] = bank[:, used:used + width]
+                middle[n, j] = bank[:, used:used + width]
                 used += width
 
-        def far_scores(n, order=(0, 1)):
-            b, h = pairs[n]
+        def far_scores(n, order):
             for j in order:
                 bank = next_bank()
-                scores(bank[:], b, 2 * h + j, 0, FIRST)
+                scores(bank[:], n, j, 0, FAR)
                 far[n, j] = bank
 
-        def mask_diag(n):
-            nc.vector.scalar_tensor_tensor(out=neg[n][:, :, S - P:], in0=diag[n][:, :2 * P].rearrange("p (j c) -> p j c", j=2),
+        def mask_diagonal(n):
+            nc.vector.scalar_tensor_tensor(out=neg[n][:, :, S - P:],
+                                           in0=diagonal[n][:, :2 * P].rearrange("p (j c) -> p j c", j=2),
                                            scalar=NEG_SCALE, in1=mask[:], op0=ALU.mult, op1=ALU.max)
 
-        def min_diag(n):
-            nc.vector.tensor_reduce(out=low[n][:, 0, :], in_=neg[n][:, :, S - P:], axis=mybir.AxisListType.X, op=ALU.min)
+        def least_diagonal(n):
+            nc.vector.tensor_reduce(out=least[n][:, 0, :], in_=neg[n][:, :, S - P:],
+                                    axis=mybir.AxisListType.X, op=ALU.min)
 
-        def min_mid(n, j):
-            start = S - seen(n, j) + FIRST
-            nc.vector.tensor_scalar(out=neg[n][:, j, start:S - P], in0=mid[n, j], scalar1=NEG_SCALE,
-                                    scalar2=low[n][:, 0, j:j + 1], op0=ALU.mult, op1=ALU.min,
-                                    accum_out=low[n][:, 1, j:j + 1])
+        def take_middle(n, j):
+            start = S - seen(n, j) + FAR
+            nc.vector.tensor_scalar(out=neg[n][:, j, start:S - P], in0=middle[n, j], scalar1=NEG_SCALE,
+                                    scalar2=least[n][:, 0, j:j + 1], op0=ALU.mult, op1=ALU.min,
+                                    accum_out=least[n][:, 1, j:j + 1])
 
-        def min_far(n, j):
-            start = S - seen(n, j)
-            before = 1 if (n, j) in mid else 0
-            nc.vector.tensor_scalar(out=neg[n][:, j, start:start + FIRST], in0=far[n, j][:], scalar1=NEG_SCALE,
-                                    scalar2=low[n][:, before, j:j + 1], op0=ALU.mult, op1=ALU.min,
-                                    accum_out=low[n][:, 2, j:j + 1])
+        def take_far_and_exp(n, j):
+            width = seen(n, j)
+            start = S - width
+            stage_before = 1 if (n, j) in middle else 0
+            nc.vector.tensor_scalar(out=neg[n][:, j, start:start + FAR], in0=far[n, j][:], scalar1=NEG_SCALE,
+                                    scalar2=least[n][:, stage_before, j:j + 1], op0=ALU.mult, op1=ALU.min,
+                                    accum_out=least[n][:, 2, j:j + 1])
+            nc.scalar.activation(out=prob[n][:, j, :width], in_=neg[n][:, j, start:], func=ACT.Exp, scale=-1.0,
+                                 bias=least[n][:, 2, j:j + 1], accum_out=total[n][:, j:j + 1])
 
-        def exp(n, j):
-            w = seen(n, j)
-            nc.scalar.activation(out=prob[n][:, j, :w], in_=neg[n][:, j, S - w:], func=ACT.Exp, scale=-1.0,
-                                 bias=low[n][:, 2, j:j + 1], accum_out=total[n][:, j:j + 1])
+        def invert(n, j):
+            nc.vector.reciprocal(out=inverse[n][:, j:j + 1], in_=total[n][:, j:j + 1])
 
-        def invert(n, js):
-            nc.vector.reciprocal(out=inv[n][:, js], in_=total[n][:, js])
+        def on_gpsimd(row, factor):
+            nc.gpsimd.tensor_scalar(out=row, in0=row, scalar1=factor, scalar2=0.0, op0=ALU.mult, op1=ALU.add)
 
-        def finish(n, j, on_vector=False):
-            b, h = pairs[n]
-            w = seen(n, j)
-            row = prob[n][:, j, :w]
-            if on_vector:
-                nc.vector.tensor_scalar(out=row, in0=row, scalar1=inv[n][:, j:j + 1], scalar2=None, op0=ALU.mult)
-            else:
-                nc.gpsimd.tensor_scalar(out=row, in0=row, scalar1=inv[n][:, j:j + 1], scalar2=0.0,
-                                        op0=ALU.mult, op1=ALU.add)
-            i = 2 * h + j
-            nc.sync.dma_start(out=out[b, i * P:(i + 1) * P, :w], in_=row)
+        def on_vector(row, factor):
+            nc.vector.tensor_scalar(out=row, in0=row, scalar1=factor, scalar2=None, op0=ALU.mult)
 
-        both = slice(0, 2)
-        turn(0, on_vector=True)
-        turn(1)
+        def on_scalar(row, factor):
+            nc.scalar.activation(out=row, in_=row, func=ACT.Copy, scale=factor)
+
+        def finish(n, j, normalise, half=None):
+            b, part = PAIRS[n]
+            width = seen(n, j)
+            cols = slice(0, width) if half is None else slice(half * width // 2, (half + 1) * width // 2)
+            row = prob[n][:, j, cols]
+            normalise(row, inverse[n][:, j:j + 1])
+            first = part * CHUNK + j * P
+            nc.sync.dma_start(out=out[b, first:first + P, cols], in_=row)
+
+        transpose_chunk(0, nc.vector.tensor_copy)
+        transpose_chunk(1, nc.scalar.copy)
         quantize(0)
-        turn(2)
+        transpose_chunk(2, nc.scalar.copy)
         quantize(1)
-        turn(3)
+        transpose_chunk(3, nc.scalar.copy)
         quantize(2)
-        turn(4)
+        transpose_chunk(4, nc.scalar.copy)
         near_scores(0)
         quantize(3)
         far_scores(0, (0,))
         far_scores(0, (1,))
-        mask_diag(0)
+        mask_diagonal(0)
         quantize(4)
-        min_diag(0)
-        turn(5)
-        turn(6)
-        turn(7)
-        min_mid(0, 1)
-        min_far(0, 0)
-        exp(0, 0)
-        min_far(0, 1)
-        exp(0, 1)
+        least_diagonal(0)
+        transpose_chunk(5, nc.scalar.copy)
+        transpose_chunk(6, nc.scalar.copy)
+        transpose_chunk(7, nc.scalar.copy)
+        take_middle(0, 1)
+        take_far_and_exp(0, 0)
+        take_far_and_exp(0, 1)
         quantize(5)
         near_scores(1)
         far_scores(1, (0,))
         far_scores(1, (1,))
         quantize(6)
-        mask_diag(1)
+        mask_diagonal(1)
         quantize(7)
-        min_diag(1)
-        invert(0, slice(0, 1))
-        finish(0, 0)
-        turn(8)
-        turn(9)
-        turn(10)
-        turn(11)
-        min_mid(1, 0)
-        min_mid(1, 1)
-        invert(0, slice(1, 2))
-        finish(0, 1)
-        min_far(1, 0)
-        exp(1, 0)
-        min_far(1, 1)
-        exp(1, 1)
+        least_diagonal(1)
+        invert(0, 0)
+        finish(0, 0, on_gpsimd)
+        transpose_chunk(8, nc.scalar.copy)
+        transpose_chunk(9, nc.scalar.copy)
+        transpose_chunk(10, nc.scalar.copy)
+        transpose_chunk(11, nc.scalar.copy)
+        take_middle(1, 0)
+        take_middle(1, 1)
+        invert(0, 1)
+        finish(0, 1, on_gpsimd, half=0)
+        take_far_and_exp(1, 0)
+        take_far_and_exp(1, 1)
+        finish(0, 1, on_vector, half=1)
         quantize(8)
         near_scores(2)
         quantize(9)
         quantize(10)
         far_scores(2, (0,))
         far_scores(2, (1,))
-        mask_diag(2)
+        mask_diagonal(2)
         quantize(11)
         near_scores(3)
-        min_diag(2)
-        invert(1, slice(0, 1))
-        finish(1, 0)
-        min_mid(2, 0)
-        min_mid(2, 1)
-        invert(1, slice(1, 2))
-        finish(1, 1)
-        min_far(2, 0)
-        exp(2, 0)
-        mask_diag(3)
-        min_far(2, 1)
-        exp(2, 1)
-        min_diag(3)
+        least_diagonal(2)
+        invert(1, 0)
+        finish(1, 0, on_gpsimd, half=0)
+        take_middle(2, 0)
+        take_middle(2, 1)
+        invert(1, 1)
+        finish(1, 0, on_scalar, half=1)
+        finish(1, 1, on_scalar, half=1)
+        finish(1, 1, on_gpsimd, half=0)
+        take_far_and_exp(2, 0)
+        mask_diagonal(3)
+        take_far_and_exp(2, 1)
+        least_diagonal(3)
         far_scores(3, (1,))
         far_scores(3, (0,))
-        invert(2, slice(0, 1))
-        finish(2, 0)
-        min_mid(3, 1)
-        min_far(3, 0)
-        exp(3, 0)
-        min_far(3, 1)
-        exp(3, 1)
-        invert(2, slice(1, 2))
-        finish(2, 1, on_vector=True)
-        invert(3, slice(0, 1))
-        finish(3, 0, on_vector=True)
-        invert(3, slice(1, 2))
-        finish(3, 1, on_vector=True)
+        invert(2, 0)
+        finish(2, 0, on_gpsimd, half=0)
+        take_middle(3, 1)
+        take_far_and_exp(3, 0)
+        finish(2, 0, on_vector, half=1)
+        invert(2, 1)
+        finish(2, 1, on_gpsimd, half=0)
+        take_far_and_exp(3, 1)
+        finish(2, 1, on_vector, half=1)
+        invert(3, 0)
+        finish(3, 0, on_vector)
+        invert(3, 1)
+        finish(3, 1, on_vector)

import math
from contextlib import ExitStack

import concourse.mybir as mybir
from concourse.masks import make_identity

B, S, E, Q = 2, 1024, 512, 512
FLOPS = 2 * B * Q * S * E

P = 128
CHUNK = 256
FAR = S - Q
BANK = 512
N_BANKS = 8
HUGE = 2.0 ** 127
NEG_SCALE = -1.0 / math.sqrt(E)

F32 = mybir.dt.float32
BF16 = mybir.dt.bfloat16
U32 = mybir.dt.uint32
U8 = mybir.dt.uint8
FORMAT = {"q": mybir.dt.float8_e5m2_x4, "k": mybir.dt.float8_e4m3fn_x4}
ALU = mybir.AluOpType
ACT = mybir.ActivationFunctionType

PAIRS = [(0, 0), (0, 1), (1, 1), (1, 0)]
CHUNKS = [("q", 0, 0), ("k", 0, 2), ("k", 0, 0), ("k", 0, 1),
          ("q", 0, 1), ("k", 0, 3),
          ("q", 1, 1), ("k", 1, 3), ("k", 1, 2), ("k", 1, 0), ("k", 1, 1),
          ("q", 1, 0)]


def seen(n, j):
    return FAR + (2 * PAIRS[n][1] + j + 1) * P


def tile_rawattention_pb_kernel(tc, q_rot, k_rot, out):
    nc = tc.nc
    with ExitStack() as ctx:
        keep = ctx.enter_context(tc.tile_pool(name="keep", bufs=1))
        psum = ctx.enter_context(tc.psum_pool(name="psum", bufs=1))
        ctx.enter_context(tc.manual_schedule())

        def next_bank():
            bank = psum.tile([P, BANK], F32, name="bank", bufs=N_BANKS)
            return bank

        raw = []
        for c, (kind, b, part) in enumerate(CHUNKS):
            rows = (q_rot if kind == "q" else k_rot)[b, part * CHUNK:(part + 1) * CHUNK, :]
            loaded = keep.tile([P, 2, E], BF16, name="raw%d" % c)
            nc.sync.dma_start(out=loaded[:], in_=rows.rearrange("(p r) e -> p r e", r=2))
            raw.append(loaded)

        ident = keep.tile([P, P], F32, name="ident")
        make_identity(nc, ident[:])
        mask = keep.tile([P, 2, P], F32, name="mask")
        nc.gpsimd.memset(mask[:], -HUGE)
        nc.gpsimd.affine_select(out=mask[:], in_=mask[:], pattern=[[0, 2], [-1, P]], compare_op=ALU.is_ge,
                                fill=HUGE, base=0, channel_multiplier=1)

        widest = S - FAR - P
        masked = keep.tile([P, B, widest], F32, name="masked")
        nc.vector.memset(masked[:], HUGE)
        zeros = keep.tile([P, B, widest], F32, name="zeros")
        nc.scalar.activation(out=zeros[:], in_=masked[:], func=ACT.Exp, scale=-1.0)
        for i in range(Q // P - 1):
            first_zero = FAR + (i + 1) * P
            nc.sync.dma_start(out=out[:, i * P:(i + 1) * P, first_zero:].rearrange("b p n -> p b n"),
                              in_=zeros[:, :, :S - first_zero])

        codes = {}
        scales = {}
        for b in range(B):
            for kind, n_rows in (("q", Q), ("k", S)):
                codes[kind, b] = keep.tile([P, n_rows], U32, name="codes_%s%d" % (kind, b), align_bytes=64)
                scales[kind, b] = keep.tile([P, n_rows], U8, name="scales_%s%d" % (kind, b), align_bytes=64)

        grouped = {}

        def transpose_chunk(c, copy):
            words = raw[c][:].bitcast(F32)
            bank = next_bank()
            for r in range(2):
                for u in range(2):
                    slot = 2 * r + u
                    nc.tensor.transpose(bank[:, slot * P:(slot + 1) * P], words[:, r, u::2], ident[:])
            turned = keep.tile([P, 4 * CHUNK], BF16, name="grouped%d" % c, align_bytes=64)
            copy(out=turned[:].bitcast(F32).rearrange("p (m slot) -> p m slot", slot=4),
                 in_=bank[:].rearrange("p (slot m) -> p m slot", slot=4))
            grouped[c] = turned

        def quantize(c):
            kind, b, part = CHUNKS[c]
            cols = slice(part * CHUNK, (part + 1) * CHUNK)
            nc.vector.quantize_mx(out=codes[kind, b][:, cols].bitcast(FORMAT[kind]),
                                  scales=scales[kind, b][:, cols], in_=grouped[c][:])

        def scores(dst, n, j, key0, width):
            b, part = PAIRS[n]
            queries = slice(part * CHUNK + j * P, part * CHUNK + (j + 1) * P)
            keys = slice(key0, key0 + width)
            nc.tensor.matmul_mx(out=dst,
                                lhsT=codes["q", b][:, queries].bitcast(FORMAT["q"]),
                                lhsT_scale=scales["q", b][:, queries],
                                rhs=codes["k", b][:, keys].bitcast(FORMAT["k"]),
                                rhs_scale=scales["k", b][:, keys],
                                start=True, stop=True)

        pairs = range(len(PAIRS))
        neg = [keep.tile([P, 2, S], F32, name="neg%d" % n) for n in pairs]
        prob = [keep.tile([P, 2, S], F32, name="prob%d" % n) for n in pairs]
        least = [keep.tile([P, 3, 2], F32, name="least%d" % n) for n in pairs]
        total = [keep.tile([P, 2], F32, name="total%d" % n) for n in pairs]
        inverse = [keep.tile([P, 2], F32, name="inverse%d" % n) for n in pairs]
        diagonal, middle, far = {}, {}, {}

        def near_scores(n):
            bank = next_bank()
            for j in range(2):
                scores(bank[:, j * P:(j + 1) * P], n, j, seen(n, j) - P, P)
            diagonal[n] = bank
            used = 2 * P
            for j in range(2):
                width = seen(n, j) - P - FAR
                if width == 0:
                    continue
                if used + width > BANK:
                    bank = next_bank()
                    used = 0
                done = 0
                for piece in (2 * P, P):
                    if width - done >= piece:
                        scores(bank[:, used + done:used + done + piece], n, j, FAR + done, piece)
                        done += piece
                middle[n, j] = bank[:, used:used + width]
                used += width

        def far_scores(n, order):
            for j in order:
                bank = next_bank()
                scores(bank[:], n, j, 0, FAR)
                far[n, j] = bank

        def mask_diagonal(n):
            nc.vector.scalar_tensor_tensor(out=neg[n][:, :, S - P:],
                                           in0=diagonal[n][:, :2 * P].rearrange("p (j c) -> p j c", j=2),
                                           scalar=NEG_SCALE, in1=mask[:], op0=ALU.mult, op1=ALU.max)

        def least_diagonal(n):
            nc.vector.tensor_reduce(out=least[n][:, 0, :], in_=neg[n][:, :, S - P:],
                                    axis=mybir.AxisListType.X, op=ALU.min)

        def take_middle(n, j):
            start = S - seen(n, j) + FAR
            nc.vector.tensor_scalar(out=neg[n][:, j, start:S - P], in0=middle[n, j], scalar1=NEG_SCALE,
                                    scalar2=least[n][:, 0, j:j + 1], op0=ALU.mult, op1=ALU.min,
                                    accum_out=least[n][:, 1, j:j + 1])

        def take_far_and_exp(n, j):
            width = seen(n, j)
            start = S - width
            stage_before = 1 if (n, j) in middle else 0
            nc.vector.tensor_scalar(out=neg[n][:, j, start:start + FAR], in0=far[n, j][:], scalar1=NEG_SCALE,
                                    scalar2=least[n][:, stage_before, j:j + 1], op0=ALU.mult, op1=ALU.min,
                                    accum_out=least[n][:, 2, j:j + 1])
            nc.scalar.activation(out=prob[n][:, j, :width], in_=neg[n][:, j, start:], func=ACT.Exp, scale=-1.0,
                                 bias=least[n][:, 2, j:j + 1], accum_out=total[n][:, j:j + 1])

        def invert(n, j):
            nc.vector.reciprocal(out=inverse[n][:, j:j + 1], in_=total[n][:, j:j + 1])

        def on_gpsimd(row, factor):
            nc.gpsimd.tensor_scalar(out=row, in0=row, scalar1=factor, scalar2=0.0, op0=ALU.mult, op1=ALU.add)

        def on_vector(row, factor):
            nc.vector.tensor_scalar(out=row, in0=row, scalar1=factor, scalar2=None, op0=ALU.mult)

        def on_scalar(row, factor):
            nc.scalar.activation(out=row, in_=row, func=ACT.Copy, scale=factor)

        def finish(n, j, normalise, half=None):
            b, part = PAIRS[n]
            width = seen(n, j)
            cols = slice(0, width) if half is None else slice(half * width // 2, (half + 1) * width // 2)
            row = prob[n][:, j, cols]
            normalise(row, inverse[n][:, j:j + 1])
            first = part * CHUNK + j * P
            nc.sync.dma_start(out=out[b, first:first + P, cols], in_=row)

        transpose_chunk(0, nc.vector.tensor_copy)
        transpose_chunk(1, nc.scalar.copy)
        quantize(0)
        transpose_chunk(2, nc.scalar.copy)
        quantize(1)
        transpose_chunk(3, nc.scalar.copy)
        quantize(2)
        transpose_chunk(4, nc.scalar.copy)
        near_scores(0)
        quantize(3)
        far_scores(0, (0,))
        far_scores(0, (1,))
        mask_diagonal(0)
        quantize(4)
        least_diagonal(0)
        transpose_chunk(5, nc.scalar.copy)
        transpose_chunk(6, nc.scalar.copy)
        transpose_chunk(7, nc.scalar.copy)
        take_middle(0, 1)
        take_far_and_exp(0, 0)
        take_far_and_exp(0, 1)
        quantize(5)
        near_scores(1)
        far_scores(1, (0,))
        far_scores(1, (1,))
        quantize(6)
        mask_diagonal(1)
        quantize(7)
        least_diagonal(1)
        invert(0, 0)
        finish(0, 0, on_gpsimd)
        transpose_chunk(8, nc.scalar.copy)
        transpose_chunk(9, nc.scalar.copy)
        transpose_chunk(10, nc.scalar.copy)
        transpose_chunk(11, nc.scalar.copy)
        take_middle(1, 0)
        take_middle(1, 1)
        invert(0, 1)
        finish(0, 1, on_gpsimd, half=0)
        take_far_and_exp(1, 0)
        take_far_and_exp(1, 1)
        finish(0, 1, on_vector, half=1)
        quantize(8)
        near_scores(2)
        quantize(9)
        quantize(10)
        far_scores(2, (0,))
        far_scores(2, (1,))
        mask_diagonal(2)
        quantize(11)
        near_scores(3)
        least_diagonal(2)
        invert(1, 0)
        finish(1, 0, on_gpsimd, half=0)
        take_middle(2, 0)
        take_middle(2, 1)
        invert(1, 1)
        finish(1, 0, on_scalar, half=1)
        finish(1, 1, on_scalar, half=1)
        finish(1, 1, on_gpsimd, half=0)
        take_far_and_exp(2, 0)
        mask_diagonal(3)
        take_far_and_exp(2, 1)
        least_diagonal(3)
        far_scores(3, (1,))
        far_scores(3, (0,))
        invert(2, 0)
        finish(2, 0, on_gpsimd, half=0)
        take_middle(3, 1)
        take_far_and_exp(3, 0)
        finish(2, 0, on_vector, half=1)
        invert(2, 1)
        finish(2, 1, on_gpsimd, half=0)
        take_far_and_exp(3, 1)
        finish(2, 1, on_vector, half=1)
        invert(3, 0)
        finish(3, 0, on_vector)
        invert(3, 1)
        finish(3, 1, on_vector)
